import numpy as np
import ml_dtypes

BF16 = ml_dtypes.bfloat16


def bf(x):
    return np.asarray(x, np.float32).astype(BF16)


def f32(x):
    return np.asarray(x, np.float32)


def f64(x):
    return np.asarray(x).astype(np.float64)


def striped(idx):
    return np.tile(idx.reshape(-1, 16).T, (8, 1))


D, HOPS, C, Q, S, N = 128, 3, 768, 1024, 4096, 2048


def setup_inputs():
    return {"time_tab": f32(0.5 * np.random.standard_normal((C, S))), "mems": f32(0.5 * np.random.standard_normal((C, N))), "u0": f32(0.25 * np.random.standard_normal((D, Q))), "offs": striped(np.random.permutation(S)[:N])}


def reference(time_tab, mems, u0, offs):
    idx = offs[:16].T.reshape(-1)
    mem = (f64(time_tab)[:, idx] + f64(mems)).reshape(HOPS, -1, D, N)
    u = f64(u0)
    for i in range(HOPS):
        logit = u.T @ mem[i, 0]
        e = np.exp(logit - logit.max(axis=1, keepdims=True))
        p = e / e.sum(axis=1, keepdims=True)
        u = u + mem[i, 1] @ p.T
    return u

@@ -1,0 +1,161 @@
+from contextlib import ExitStack
+
+import concourse.mybir as mybir
+from concourse.masks import make_identity
+
+F32 = mybir.dt.float32
+BF16 = mybir.dt.bfloat16
+U16 = mybir.dt.uint16
+ADD = mybir.AluOpType.add
+MAX = mybir.AluOpType.max
+EXP = mybir.ActivationFunctionType.Exp
+COPY = mybir.ActivationFunctionType.Copy
+ALONG_ROW = mybir.AxisListType.X
+
+P = 128
+HOPS = 3
+Q = 1024
+S = 4096
+N = 2048
+BANK = 512
+PIECES = N // BANK
+SLOT_BLOCKS = N // P
+BLOCKS_IN_PIECE = BANK // P
+Q_BLOCKS = Q // P
+OFFS_IN_COLUMN = 16
+VALUE_WIDTH = P + 2
+
+FLOPS = HOPS * 2 * (2 * P * N * Q)
+
+
+def tile_base_b_kernel(tc, time_tab, mems, u0, offs, out):
+    nc = tc.nc
+    with ExitStack() as ctx:
+        held = ctx.enter_context(tc.tile_pool(name="held", bufs=1))
+        work = ctx.enter_context(tc.tile_pool(name="work", bufs=2))
+        stats = ctx.enter_context(tc.tile_pool(name="stats", bufs=4))
+        psum_logit = ctx.enter_context(tc.psum_pool(name="psum_logit", bufs=PIECES))
+        psum_flip = ctx.enter_context(tc.psum_pool(name="psum_flip", bufs=2))
+        psum_read = ctx.enter_context(tc.psum_pool(name="psum_read", bufs=1))
+        psum_turn = ctx.enter_context(tc.psum_pool(name="psum_turn", bufs=1))
+
+        offsets = held.tile([P, N // OFFS_IN_COLUMN], U16, name="offsets")
+        nc.sync.dma_start(offsets[:], offs)
+        u = held.tile([P, Q], F32, name="u")
+        tables = []
+        slots = []
+        for block in range(2 * HOPS):
+            rows = slice(block * P, (block + 1) * P)
+            table = held.tile([P, S], F32, name="table%d" % block)
+            nc.sync.dma_start(table[:], time_tab[rows, :])
+            slot = held.tile([P, N], F32, name="slot%d" % block)
+            nc.sync.dma_start(slot[:], mems[rows, :])
+            tables.append(table)
+            slots.append(slot)
+            if block == 0:
+                nc.sync.dma_start(u[:], u0)
+
+        ident_bf = held.tile([P, P], BF16, name="ident_bf")
+        make_identity(nc, ident_bf[:])
+        ident_f = held.tile([P, P], F32, name="ident_f")
+        make_identity(nc, ident_f[:])
+
+        keys = [held.tile([P, N], BF16, name="keys%d" % i) for i in range(HOPS)]
+        values_t = [held.tile([P, SLOT_BLOCKS, VALUE_WIDTH], BF16, name="values_t%d" % i) for i in range(HOPS)]
+        for i in range(HOPS):
+            nc.gpsimd.memset(values_t[i][:], 1.0)
+
+        u_bf = held.tile([P, Q], BF16, name="u_bf")
+        nc.scalar.copy(u_bf[:], u[:])
+
+        def look_up_and_add(block, piece):
+            columns = slice(piece * BANK, (piece + 1) * BANK)
+            first = piece * BANK // OFFS_IN_COLUMN
+            mem = work.tile([P, BANK], F32, name="mem", bufs=3)
+            nc.vector.tensor_tensor(
+                mem[:],
+                tables[block][:].indirect(offsets[:, first : first + BANK // OFFS_IN_COLUMN]),
+                slots[block][:, columns],
+                ADD,
+            )
+            return mem
+
+        def prepare_keys(i, piece):
+            mem = look_up_and_add(2 * i, piece)
+            nc.scalar.copy(keys[i][:, piece * BANK : (piece + 1) * BANK], mem[:])
+
+        def prepare_values(i, piece):
+            mem = look_up_and_add(2 * i + 1, piece)
+            turned = psum_turn.tile([P, BANK], F32, name="turned", tag="turn")
+            for b in range(BLOCKS_IN_PIECE):
+                nc.tensor.transpose(turned[:, b * P : (b + 1) * P], mem[:, b * P : (b + 1) * P], ident_f[:])
+            first = piece * BLOCKS_IN_PIECE
+            nc.scalar.copy(
+                values_t[i][:, first : first + BLOCKS_IN_PIECE, 0:P],
+                turned[:].rearrange("p (b d) -> p b d", b=BLOCKS_IN_PIECE),
+            )
+
+        def prepare(i, step):
+            if step < PIECES:
+                prepare_keys(i, step)
+            else:
+                prepare_values(i, step - PIECES)
+
+        def attend(i, qb):
+            qs = slice(qb * P, (qb + 1) * P)
+            logits = []
+            piece_max = stats.tile([P, PIECES], F32, name="piece_max")
+            for piece in range(PIECES):
+                logit = psum_logit.tile([P, BANK], F32, name="logit", tag="logit")
+                nc.tensor.matmul(
+                    logit[:], u_bf[:, qs], keys[i][:, piece * BANK : (piece + 1) * BANK], start=True, stop=True
+                )
+                nc.vector.tensor_reduce(piece_max[:, piece : piece + 1], logit[:], axis=ALONG_ROW, op=MAX)
+                logits.append(logit)
+            neg_max = stats.tile([P, 1], F32, name="neg_max")
+            nc.vector.tensor_reduce(neg_max[:], piece_max[:], axis=ALONG_ROW, op=MAX, negate=True)
+
+            weights = work.tile([P, N], BF16, name="weights")
+            for piece in range(PIECES):
+                nc.scalar.activation(
+                    weights[:, piece * BANK : (piece + 1) * BANK], logits[piece][:], EXP, bias=neg_max[:], scale=1.0
+                )
+
+            weights_t = work.tile([P, N], BF16, name="weights_t")
+            half = SLOT_BLOCKS // 2
+            for h in range(2):
+                flipped = psum_flip.tile([P, half * P], BF16, name="flipped")
+                for b in range(half):
+                    jb = h * half + b
+                    nc.tensor.transpose(flipped[:, b * P : (b + 1) * P], weights[:, jb * P : (jb + 1) * P], ident_bf[:])
+                nc.scalar.copy(weights_t[:, h * half * P : (h + 1) * half * P], flipped[:])
+
+            read = psum_read.tile([P, VALUE_WIDTH], F32, name="read")
+            for jb in range(SLOT_BLOCKS):
+                nc.tensor.matmul(
+                    read[:],
+                    weights_t[:, jb * P : (jb + 1) * P],
+                    values_t[i][:, jb, :],
+                    start=(jb == 0),
+                    stop=(jb == SLOT_BLOCKS - 1),
+                )
+            inv_sum = stats.tile([P, 1], F32, name="inv_sum")
+            nc.vector.reciprocal(inv_sum[:], read[:, P : P + 1])
+            answer = work.tile([P, P], F32, name="answer")
+            nc.scalar.activation(answer[:], read[:, 0:P], COPY, scale=inv_sum[:])
+
+            answer_t = psum_turn.tile([P, P], F32, name="answer_t", tag="turn")
+            nc.tensor.transpose(answer_t[:], answer[:], ident_f[:])
+            nc.vector.tensor_tensor(u[:, qs], answer_t[:], u[:, qs], ADD)
+            if i + 1 < HOPS:
+                nc.scalar.copy(u_bf[:, qs], u[:, qs])
+            else:
+                nc.sync.dma_start(out[:, qs], u[:, qs])
+
+        for step in range(2 * PIECES):
+            prepare(0, step)
+        for i in range(HOPS):
+            for qb in range(Q_BLOCKS):
+                attend(i, qb)
+                if i + 1 < HOPS:
+                    prepare(i + 1, qb)

@@ -8,6 +8,7 @@ BF16 = mybir.dt.bfloat16
 U16 = mybir.dt.uint16
 ADD = mybir.AluOpType.add
 MAX = mybir.AluOpType.max
+MULT = mybir.AluOpType.mult
 EXP = mybir.ActivationFunctionType.Exp
 COPY = mybir.ActivationFunctionType.Copy
 ALONG_ROW = mybir.AxisListType.X
@@ -32,10 +33,10 @@ def tile_base_b_kernel(tc, time_tab, mems, u0, offs, out):
     nc = tc.nc
     with ExitStack() as ctx:
         held = ctx.enter_context(tc.tile_pool(name="held", bufs=1))
-        work = ctx.enter_context(tc.tile_pool(name="work", bufs=2))
+        work = ctx.enter_context(tc.tile_pool(name="work", bufs=3))
         stats = ctx.enter_context(tc.tile_pool(name="stats", bufs=4))
-        psum_logit = ctx.enter_context(tc.psum_pool(name="psum_logit", bufs=PIECES))
-        psum_flip = ctx.enter_context(tc.psum_pool(name="psum_flip", bufs=2))
+        psum_logit = ctx.enter_context(tc.psum_pool(name="psum_logit", bufs=3))
+        psum_flip = ctx.enter_context(tc.psum_pool(name="psum_flip", bufs=3))
         psum_read = ctx.enter_context(tc.psum_pool(name="psum_read", bufs=1))
         psum_turn = ctx.enter_context(tc.psum_pool(name="psum_turn", bufs=1))
 
@@ -71,7 +72,7 @@ def tile_base_b_kernel(tc, time_tab, mems, u0, offs, out):
         def look_up_and_add(block, piece):
             columns = slice(piece * BANK, (piece + 1) * BANK)
             first = piece * BANK // OFFS_IN_COLUMN
-            mem = work.tile([P, BANK], F32, name="mem", bufs=3)
+            mem = work.tile([P, BANK], F32, name="mem")
             nc.vector.tensor_tensor(
                 mem[:],
                 tables[block][:].indirect(offsets[:, first : first + BANK // OFFS_IN_COLUMN]),
@@ -103,23 +104,20 @@ def tile_base_b_kernel(tc, time_tab, mems, u0, offs, out):
 
         def attend(i, qb):
             qs = slice(qb * P, (qb + 1) * P)
-            logits = []
+            logits = work.tile([P, N], F32, name="logits")
             piece_max = stats.tile([P, PIECES], F32, name="piece_max")
             for piece in range(PIECES):
-                logit = psum_logit.tile([P, BANK], F32, name="logit", tag="logit")
-                nc.tensor.matmul(
-                    logit[:], u_bf[:, qs], keys[i][:, piece * BANK : (piece + 1) * BANK], start=True, stop=True
+                columns = slice(piece * BANK, (piece + 1) * BANK)
+                logit = psum_logit.tile([P, BANK], F32, name="logit")
+                nc.tensor.matmul(logit[:], u_bf[:, qs], keys[i][:, columns], start=True, stop=True)
+                nc.vector.tensor_scalar(
+                    logits[:, columns], logit[:], 1.0, None, MULT, MAX, accum_out=piece_max[:, piece : piece + 1]
                 )
-                nc.vector.tensor_reduce(piece_max[:, piece : piece + 1], logit[:], axis=ALONG_ROW, op=MAX)
-                logits.append(logit)
             neg_max = stats.tile([P, 1], F32, name="neg_max")
             nc.vector.tensor_reduce(neg_max[:], piece_max[:], axis=ALONG_ROW, op=MAX, negate=True)
 
             weights = work.tile([P, N], BF16, name="weights")
-            for piece in range(PIECES):
-                nc.scalar.activation(
-                    weights[:, piece * BANK : (piece + 1) * BANK], logits[piece][:], EXP, bias=neg_max[:], scale=1.0
-                )
+            nc.scalar.activation(weights[:], logits[:], EXP, bias=neg_max[:], scale=1.0)
 
             weights_t = work.tile([P, N], BF16, name="weights_t")
             half = SLOT_BLOCKS // 2
@@ -128,7 +126,8 @@ def tile_base_b_kernel(tc, time_tab, mems, u0, offs, out):
                 for b in range(half):
                     jb = h * half + b
                     nc.tensor.transpose(flipped[:, b * P : (b + 1) * P], weights[:, jb * P : (jb + 1) * P], ident_bf[:])
-                nc.scalar.copy(weights_t[:, h * half * P : (h + 1) * half * P], flipped[:])
+                copy_out = nc.vector.tensor_copy if h == 0 else nc.scalar.copy
+                copy_out(weights_t[:, h * half * P : (h + 1) * half * P], flipped[:])
 
             read = psum_read.tile([P, VALUE_WIDTH], F32, name="read")
             for jb in range(SLOT_BLOCKS):

@@ -50,7 +50,9 @@ def tile_base_b_kernel(tc, time_tab, mems, u0, offs, out):
             table = held.tile([P, S], F32, name="table%d" % block)
             nc.sync.dma_start(table[:], time_tab[rows, :])
             slot = held.tile([P, N], F32, name="slot%d" % block)
-            nc.sync.dma_start(slot[:], mems[rows, :])
+            for piece in range(PIECES):
+                columns = slice(piece * BANK, (piece + 1) * BANK)
+                nc.sync.dma_start(slot[:, columns], mems[rows, columns])
             tables.append(table)
             slots.append(slot)
             if block == 0:
@@ -126,8 +128,7 @@ def tile_base_b_kernel(tc, time_tab, mems, u0, offs, out):
                 for b in range(half):
                     jb = h * half + b
                     nc.tensor.transpose(flipped[:, b * P : (b + 1) * P], weights[:, jb * P : (jb + 1) * P], ident_bf[:])
-                copy_out = nc.vector.tensor_copy if h == 0 else nc.scalar.copy
-                copy_out(weights_t[:, h * half * P : (h + 1) * half * P], flipped[:])
+                nc.scalar.copy(weights_t[:, h * half * P : (h + 1) * half * P], flipped[:])
 
             read = psum_read.tile([P, VALUE_WIDTH], F32, name="read")
             for jb in range(SLOT_BLOCKS):

@@ -66,7 +66,7 @@ def tile_base_b_kernel(tc, time_tab, mems, u0, offs, out):
         keys = [held.tile([P, N], BF16, name="keys%d" % i) for i in range(HOPS)]
         values_t = [held.tile([P, SLOT_BLOCKS, VALUE_WIDTH], BF16, name="values_t%d" % i) for i in range(HOPS)]
         for i in range(HOPS):
-            nc.gpsimd.memset(values_t[i][:], 1.0)
+            nc.gpsimd.memset(values_t[i][:, :, P:VALUE_WIDTH], 1.0)
 
         u_bf = held.tile([P, Q], BF16, name="u_bf")
         nc.scalar.copy(u_bf[:], u[:])
@@ -83,15 +83,20 @@ def tile_base_b_kernel(tc, time_tab, mems, u0, offs, out):
             )
             return mem
 
+        def round_on_gpsimd(rounded, exact):
+            nc.gpsimd.tensor_scalar(rounded, exact, 1.0, 0.0, MULT, ADD)
+
         def prepare_keys(i, piece):
             mem = look_up_and_add(2 * i, piece)
-            nc.scalar.copy(keys[i][:, piece * BANK : (piece + 1) * BANK], mem[:])
+            round_on_gpsimd(keys[i][:, piece * BANK : (piece + 1) * BANK], mem[:])
 
         def prepare_values(i, piece):
             mem = look_up_and_add(2 * i + 1, piece)
-            turned = psum_turn.tile([P, BANK], F32, name="turned", tag="turn")
+            mem_bf = work.tile([P, BANK], BF16, name="mem_bf")
+            round_on_gpsimd(mem_bf[:], mem[:])
+            turned = psum_turn.tile([P, BANK], BF16, name="turned", tag="turn")
             for b in range(BLOCKS_IN_PIECE):
-                nc.tensor.transpose(turned[:, b * P : (b + 1) * P], mem[:, b * P : (b + 1) * P], ident_f[:])
+                nc.tensor.transpose(turned[:, b * P : (b + 1) * P], mem_bf[:, b * P : (b + 1) * P], ident_bf[:])
             first = piece * BLOCKS_IN_PIECE
             nc.scalar.copy(
                 values_t[i][:, first : first + BLOCKS_IN_PIECE, 0:P],
@@ -148,7 +153,7 @@ def tile_base_b_kernel(tc, time_tab, mems, u0, offs, out):
             nc.tensor.transpose(answer_t[:], answer[:], ident_f[:])
             nc.vector.tensor_tensor(u[:, qs], answer_t[:], u[:, qs], ADD)
             if i + 1 < HOPS:
-                nc.scalar.copy(u_bf[:, qs], u[:, qs])
+                round_on_gpsimd(u_bf[:, qs], u[:, qs])
             else:
                 nc.sync.dma_start(out[:, qs], u[:, qs])
 

@@ -147,7 +147,10 @@ def tile_base_b_kernel(tc, time_tab, mems, u0, offs, out):
             inv_sum = stats.tile([P, 1], F32, name="inv_sum")
             nc.vector.reciprocal(inv_sum[:], read[:, P : P + 1])
             answer = work.tile([P, P], F32, name="answer")
-            nc.scalar.activation(answer[:], read[:, 0:P], COPY, scale=inv_sum[:])
+            if i + 1 < HOPS:
+                nc.scalar.activation(answer[:], read[:, 0:P], COPY, scale=inv_sum[:])
+            else:
+                nc.vector.tensor_scalar(answer[:], read[:, 0:P], inv_sum[:], None, MULT)
 
             answer_t = psum_turn.tile([P, P], F32, name="answer_t", tag="turn")
             nc.tensor.transpose(answer_t[:], answer[:], ident_f[:])

@@ -25,6 +25,7 @@ BLOCKS_IN_PIECE = BANK // P
 Q_BLOCKS = Q // P
 OFFS_IN_COLUMN = 16
 VALUE_WIDTH = P + 2
+DRAIN = 2
 
 FLOPS = HOPS * 2 * (2 * P * N * Q)
 
@@ -111,6 +112,8 @@ def tile_base_b_kernel(tc, time_tab, mems, u0, offs, out):
 
         def attend(i, qb):
             qs = slice(qb * P, (qb + 1) * P)
+            last = i == HOPS - 1 and qb == Q_BLOCKS - 1
+            drain = i == HOPS - 1 and qb >= Q_BLOCKS - DRAIN
             logits = work.tile([P, N], F32, name="logits")
             piece_max = stats.tile([P, PIECES], F32, name="piece_max")
             for piece in range(PIECES):
@@ -124,16 +127,22 @@ def tile_base_b_kernel(tc, time_tab, mems, u0, offs, out):
             nc.vector.tensor_reduce(neg_max[:], piece_max[:], axis=ALONG_ROW, op=MAX, negate=True)
 
             weights = work.tile([P, N], BF16, name="weights")
-            nc.scalar.activation(weights[:], logits[:], EXP, bias=neg_max[:], scale=1.0)
+            exp_width = BANK if last else N
+            for first in range(0, N, exp_width):
+                columns = slice(first, first + exp_width)
+                nc.scalar.activation(weights[:, columns], logits[:, columns], EXP, bias=neg_max[:], scale=1.0)
 
             weights_t = work.tile([P, N], BF16, name="weights_t")
-            half = SLOT_BLOCKS // 2
-            for h in range(2):
-                flipped = psum_flip.tile([P, half * P], BF16, name="flipped")
-                for b in range(half):
-                    jb = h * half + b
+            run = BANK // P if last else 2 * BANK // P
+            for first in range(0, SLOT_BLOCKS, run):
+                flipped = psum_flip.tile([P, run * P], BF16, name="flipped")
+                for b in range(run):
+                    jb = first + b
                     nc.tensor.transpose(flipped[:, b * P : (b + 1) * P], weights[:, jb * P : (jb + 1) * P], ident_bf[:])
-                nc.scalar.copy(weights_t[:, h * half * P : (h + 1) * half * P], flipped[:])
+                if drain:
+                    nc.vector.tensor_copy(weights_t[:, first * P : (first + run) * P], flipped[:])
+                else:
+                    nc.scalar.copy(weights_t[:, first * P : (first + run) * P], flipped[:])
 
             read = psum_read.tile([P, VALUE_WIDTH], F32, name="read")
             for jb in range(SLOT_BLOCKS):

@@ -173,6 +173,6 @@ def tile_base_b_kernel(tc, time_tab, mems, u0, offs, out):
             prepare(0, step)
         for i in range(HOPS):
             for qb in range(Q_BLOCKS):
-                attend(i, qb)
                 if i + 1 < HOPS:
                     prepare(i + 1, qb)
+                attend(i, qb)

from contextlib import ExitStack

import concourse.mybir as mybir
from concourse.masks import make_identity

F32 = mybir.dt.float32
BF16 = mybir.dt.bfloat16
U16 = mybir.dt.uint16
ADD = mybir.AluOpType.add
MAX = mybir.AluOpType.max
MULT = mybir.AluOpType.mult
EXP = mybir.ActivationFunctionType.Exp
COPY = mybir.ActivationFunctionType.Copy
ALONG_ROW = mybir.AxisListType.X

P = 128
HOPS = 3
Q = 1024
S = 4096
N = 2048
BANK = 512
PIECES = N // BANK
SLOT_BLOCKS = N // P
BLOCKS_IN_PIECE = BANK // P
Q_BLOCKS = Q // P
OFFS_IN_COLUMN = 16
VALUE_WIDTH = P + 2
DRAIN = 2

FLOPS = HOPS * 2 * (2 * P * N * Q)


def tile_base_b_kernel(tc, time_tab, mems, u0, offs, out):
    nc = tc.nc
    with ExitStack() as ctx:
        held = ctx.enter_context(tc.tile_pool(name="held", bufs=1))
        work = ctx.enter_context(tc.tile_pool(name="work", bufs=3))
        stats = ctx.enter_context(tc.tile_pool(name="stats", bufs=4))
        psum_logit = ctx.enter_context(tc.psum_pool(name="psum_logit", bufs=3))
        psum_flip = ctx.enter_context(tc.psum_pool(name="psum_flip", bufs=3))
        psum_read = ctx.enter_context(tc.psum_pool(name="psum_read", bufs=1))
        psum_turn = ctx.enter_context(tc.psum_pool(name="psum_turn", bufs=1))

        offsets = held.tile([P, N // OFFS_IN_COLUMN], U16, name="offsets")
        nc.sync.dma_start(offsets[:], offs)
        u = held.tile([P, Q], F32, name="u")
        tables = []
        slots = []
        for block in range(2 * HOPS):
            rows = slice(block * P, (block + 1) * P)
            table = held.tile([P, S], F32, name="table%d" % block)
            nc.sync.dma_start(table[:], time_tab[rows, :])
            slot = held.tile([P, N], F32, name="slot%d" % block)
            for piece in range(PIECES):
                columns = slice(piece * BANK, (piece + 1) * BANK)
                nc.sync.dma_start(slot[:, columns], mems[rows, columns])
            tables.append(table)
            slots.append(slot)
            if block == 0:
                nc.sync.dma_start(u[:], u0)

        ident_bf = held.tile([P, P], BF16, name="ident_bf")
        make_identity(nc, ident_bf[:])
        ident_f = held.tile([P, P], F32, name="ident_f")
        make_identity(nc, ident_f[:])

        keys = [held.tile([P, N], BF16, name="keys%d" % i) for i in range(HOPS)]
        values_t = [held.tile([P, SLOT_BLOCKS, VALUE_WIDTH], BF16, name="values_t%d" % i) for i in range(HOPS)]
        for i in range(HOPS):
            nc.gpsimd.memset(values_t[i][:, :, P:VALUE_WIDTH], 1.0)

        u_bf = held.tile([P, Q], BF16, name="u_bf")
        nc.scalar.copy(u_bf[:], u[:])

        def look_up_and_add(block, piece):
            columns = slice(piece * BANK, (piece + 1) * BANK)
            first = piece * BANK // OFFS_IN_COLUMN
            mem = work.tile([P, BANK], F32, name="mem")
            nc.vector.tensor_tensor(
                mem[:],
                tables[block][:].indirect(offsets[:, first : first + BANK // OFFS_IN_COLUMN]),
                slots[block][:, columns],
                ADD,
            )
            return mem

        def round_on_gpsimd(rounded, exact):
            nc.gpsimd.tensor_scalar(rounded, exact, 1.0, 0.0, MULT, ADD)

        def prepare_keys(i, piece):
            mem = look_up_and_add(2 * i, piece)
            round_on_gpsimd(keys[i][:, piece * BANK : (piece + 1) * BANK], mem[:])

        def prepare_values(i, piece):
            mem = look_up_and_add(2 * i + 1, piece)
            mem_bf = work.tile([P, BANK], BF16, name="mem_bf")
            round_on_gpsimd(mem_bf[:], mem[:])
            turned = psum_turn.tile([P, BANK], BF16, name="turned", tag="turn")
            for b in range(BLOCKS_IN_PIECE):
                nc.tensor.transpose(turned[:, b * P : (b + 1) * P], mem_bf[:, b * P : (b + 1) * P], ident_bf[:])
            first = piece * BLOCKS_IN_PIECE
            nc.scalar.copy(
                values_t[i][:, first : first + BLOCKS_IN_PIECE, 0:P],
                turned[:].rearrange("p (b d) -> p b d", b=BLOCKS_IN_PIECE),
            )

        def prepare(i, step):
            if step < PIECES:
                prepare_keys(i, step)
            else:
                prepare_values(i, step - PIECES)

        def attend(i, qb):
            qs = slice(qb * P, (qb + 1) * P)
            last = i == HOPS - 1 and qb == Q_BLOCKS - 1
            drain = i == HOPS - 1 and qb >= Q_BLOCKS - DRAIN
            logits = work.tile([P, N], F32, name="logits")
            piece_max = stats.tile([P, PIECES], F32, name="piece_max")
            for piece in range(PIECES):
                columns = slice(piece * BANK, (piece + 1) * BANK)
                logit = psum_logit.tile([P, BANK], F32, name="logit")
                nc.tensor.matmul(logit[:], u_bf[:, qs], keys[i][:, columns], start=True, stop=True)
                nc.vector.tensor_scalar(
                    logits[:, columns], logit[:], 1.0, None, MULT, MAX, accum_out=piece_max[:, piece : piece + 1]
                )
            neg_max = stats.tile([P, 1], F32, name="neg_max")
            nc.vector.tensor_reduce(neg_max[:], piece_max[:], axis=ALONG_ROW, op=MAX, negate=True)

            weights = work.tile([P, N], BF16, name="weights")
            exp_width = BANK if last else N
            for first in range(0, N, exp_width):
                columns = slice(first, first + exp_width)
                nc.scalar.activation(weights[:, columns], logits[:, columns], EXP, bias=neg_max[:], scale=1.0)

            weights_t = work.tile([P, N], BF16, name="weights_t")
            run = BANK // P if last else 2 * BANK // P
            for first in range(0, SLOT_BLOCKS, run):
                flipped = psum_flip.tile([P, run * P], BF16, name="flipped")
                for b in range(run):
                    jb = first + b
                    nc.tensor.transpose(flipped[:, b * P : (b + 1) * P], weights[:, jb * P : (jb + 1) * P], ident_bf[:])
                if drain:
                    nc.vector.tensor_copy(weights_t[:, first * P : (first + run) * P], flipped[:])
                else:
                    nc.scalar.copy(weights_t[:, first * P : (first + run) * P], flipped[:])

            read = psum_read.tile([P, VALUE_WIDTH], F32, name="read")
            for jb in range(SLOT_BLOCKS):
                nc.tensor.matmul(
                    read[:],
                    weights_t[:, jb * P : (jb + 1) * P],
                    values_t[i][:, jb, :],
                    start=(jb == 0),
                    stop=(jb == SLOT_BLOCKS - 1),
                )
            inv_sum = stats.tile([P, 1], F32, name="inv_sum")
            nc.vector.reciprocal(inv_sum[:], read[:, P : P + 1])
            answer = work.tile([P, P], F32, name="answer")
            if i + 1 < HOPS:
                nc.scalar.activation(answer[:], read[:, 0:P], COPY, scale=inv_sum[:])
            else:
                nc.vector.tensor_scalar(answer[:], read[:, 0:P], inv_sum[:], None, MULT)

            answer_t = psum_turn.tile([P, P], F32, name="answer_t", tag="turn")
            nc.tensor.transpose(answer_t[:], answer[:], ident_f[:])
            nc.vector.tensor_tensor(u[:, qs], answer_t[:], u[:, qs], ADD)
            if i + 1 < HOPS:
                round_on_gpsimd(u_bf[:, qs], u[:, qs])
            else:
                nc.sync.dma_start(out[:, qs], u[:, qs])

        for step in range(2 * PIECES):
            prepare(0, step)
        for i in range(HOPS):
            for qb in range(Q_BLOCKS):
                if i + 1 < HOPS:
                    prepare(i + 1, qb)
                attend(i, qb)
